import numpy as np
import ml_dtypes


def mxq(x, axis, fmt="e4m3"):
    dtype, down = {"e4m3": (ml_dtypes.float8_e4m3fn, 7), "e5m2": (ml_dtypes.float8_e5m2, 14)}[fmt]
    v = np.moveaxis(np.asarray(x, np.float32).astype(ml_dtypes.bfloat16).astype(np.float64), axis, -1)
    blocks = v.reshape(v.shape[:-1] + (-1, 32))
    amax = np.abs(blocks).max(-1, keepdims=True)
    byte = np.maximum(np.where(amax > 0, np.frexp(amax)[1] - 1 + 127, 0) - down, 1)
    scale = np.exp2(byte - 127.0)
    codes = (blocks / scale).astype(np.float32).astype(dtype).astype(np.float64)
    return np.moveaxis((codes * scale).reshape(v.shape), -1, axis)


WIDE = False


def mx_kscale(k):
    if not WIDE:
        return np.ones(k)
    levels = np.array([10, -10, 5, -5, 0])
    a = np.random.permutation(np.resize(levels, k // 512 * 4)).reshape(k // 512, 4)
    idx = np.arange(k)
    return np.exp2(a[idx // 512, idx % 128 // 32])


BF16 = ml_dtypes.bfloat16


def bf(x):
    return np.asarray(x, np.float32).astype(BF16)


def f64(x):
    return np.asarray(x).astype(np.float64)


E2M1 = np.array([0.0, 0.5, 1.0, 1.5, 2.0, 3.0, 4.0, 6.0, -0.0, -0.5, -1.0, -1.5, -2.0, -3.0, -4.0, -6.0])


def pack_weight(w, fmt):
    k, n = w.shape
    w = f64(bf(w)).reshape(k // 32, 32, n)
    amax = np.abs(w).max(1)
    if fmt == "e4m3":
        byte = np.frexp(amax)[1] - 1 + 127 - 7
    else:
        mant, ex = np.frexp(amax / 6.0)
        byte = np.where(mant > 0.5, ex, ex - 1) + 127
    byte = np.clip(np.where(amax > 0, byte, 1), 1, 254)
    scaled = (w * np.exp2(127.0 - byte)[:, None, :]).reshape(k, n).astype(np.float32)
    by_word = np.ascontiguousarray(scaled.reshape(k // 512, 128, 4, n).transpose(0, 1, 3, 2))
    if fmt == "e4m3":
        words = by_word.astype(ml_dtypes.float8_e4m3fn).view(np.uint8)
    else:
        c = by_word.astype(ml_dtypes.float4_e2m1fn).view(np.uint8) & 0xF
        words = c[..., 0::2] | (c[..., 1::2] << 4)
    return np.ascontiguousarray(words), np.ascontiguousarray(byte.astype(np.uint8).reshape(k // 512, 16, n))


def unpack_weight(words, scales, fmt):
    g, p, n, _ = words.shape
    if fmt == "e4m3":
        vals = np.ascontiguousarray(words).view(ml_dtypes.float8_e4m3fn).astype(np.float64)
    else:
        nib = np.empty((g, p, n, 4), np.uint8)
        nib[..., 0::2] = words & 0xF
        nib[..., 1::2] = words >> 4
        vals = E2M1[nib]
    vals = vals * np.repeat(np.exp2(scales.astype(np.float64) - 127.0), 8, axis=1)[..., None]
    return vals.transpose(0, 1, 3, 2).reshape(g * 512, n)

def pack4(w):
    words, scales = pack_weight(w, "e2m1")
    return words.reshape(words.shape[0], 128, -1), scales


def unpack4(words, scales):
    return unpack_weight(words.reshape(words.shape[0], 128, -1, 2), scales, "e2m1")


B, C, HD, H, W = 2, 512, 128, 32, 32
N = H * W
C2 = 2 * C
C3 = 3 * C


def sigmoid(v):
    return 1.0 / (1.0 + np.exp(-v))


def setup_inputs():
    s = mx_kscale(C3)
    z = bf(np.random.standard_normal((B, C2, H, W)) * s[None, :C2, None, None])
    h = bf(np.random.standard_normal((B, C, H, W)) * s[None, C2:, None, None])
    m = bf(np.random.standard_normal((B, C, H, W)))
    wm = np.random.standard_normal((C3, C3)) * 1.5 / np.sqrt(C3) / s[None, :]
    words, scales = pack4(np.ascontiguousarray(wm.T))
    bm = bf(np.random.standard_normal(C3) * 0.3)
    return {
        "z": z,
        "h": h,
        "m": m,
        "Wm_words": words,
        "Wm_scales": scales,
        "bm": bm,
    }


def reference(z, h, m, Wm_words, Wm_scales, bm):
    x = np.concatenate([f64(z), f64(h)], axis=1).reshape(B, C3, N)
    combined = ((unpack4(Wm_words, Wm_scales).T @ mxq(x, 1, "e4m3")) + f64(bm)[None, :, None]).reshape(B, C3, H, W)
    mo, mg, mi = combined[:, :C], combined[:, C:C2], combined[:, C2:]
    mi = sigmoid(mi)
    new_m = (1.0 - mi) * f64(m) + mi * np.tanh(mg)
    new_h = sigmoid(mo) * new_m
    return new_h, new_m

@@ -1,0 +1,183 @@
+from contextlib import ExitStack
+
+import concourse.mybir as mybir
+from concourse.masks import make_identity
+
+BF16 = mybir.dt.bfloat16
+F32 = mybir.dt.float32
+I32 = mybir.dt.int32
+U8 = mybir.dt.uint8
+U32 = mybir.dt.uint32
+FP8X4 = mybir.dt.float8_e4m3fn_x4
+FP4X4 = mybir.dt.float4_e2m1fn_x4
+ACT = mybir.ActivationFunctionType
+ALU = mybir.AluOpType
+
+P = 128
+PACK = 4
+K_PASS = P * PACK
+BATCH = 2
+C = 512
+PIXELS = 1024
+K_GROUPS = 3
+BLOCK = 512
+HALVES = PIXELS // BLOCK
+QUARTERS = BATCH * HALVES
+ROW_TILES = C // P
+UNITS = QUARTERS * ROW_TILES
+GATE_O, GATE_G, GATE_I = 0, 1, 2
+RUN = 4
+
+SCALAR_PIXELS_START = 176
+SCALAR_PIXELS = 384
+
+FLOPS = 2 * (3 * C) * (3 * C) * BATCH * PIXELS
+
+
+def tile_self_attention_memory_module_pb_kernel(
+    tc, z, h, m, Wm_words, Wm_scales, bm, out_0, out_1
+):
+    nc = tc.nc
+    with ExitStack() as ctx:
+        keep = ctx.enter_context(tc.tile_pool(name="keep", bufs=1))
+        group_pool = ctx.enter_context(tc.tile_pool(name="group", bufs=3))
+        gate_pool = ctx.enter_context(tc.tile_pool(name="gate", bufs=4))
+        psum = ctx.enter_context(tc.psum_pool(name="psum", bufs=8))
+
+        x_raw = [
+            [keep.tile([P, PACK, PIXELS], BF16, name="x_raw_%d_%d" % (b, g)) for g in range(K_GROUPS)]
+            for b in range(BATCH)
+        ]
+        m_sb = [keep.tile([P, ROW_TILES, PIXELS], BF16, name="m_sb_%d" % b) for b in range(BATCH)]
+        x_codes = keep.tile([P, QUARTERS * K_GROUPS, BLOCK], U32, align_bytes=64)
+        x_scales = keep.tile([P, QUARTERS * K_GROUPS, BLOCK], U8, align_bytes=64)
+        w_words = keep.tile([P, K_GROUPS, 2 * 3 * C], U8, align_bytes=64)
+        w_scales = keep.tile([P, K_GROUPS, 3 * C], U8, align_bytes=64)
+        bias_rows = keep.tile([P, P], BF16)
+        identity = keep.tile([P, P], BF16)
+        bias = keep.tile([P, 3 * ROW_TILES], F32)
+        warm = keep.tile([P, 2], F32)
+
+        nc.vector.memset(w_scales[:].bitcast(I32), 0)
+        nc.vector.memset(bias_rows[:], 0.0)
+        nc.vector.memset(warm[:, 0:1], 0.0)
+        nc.scalar.activation(out=warm[:, 1:2], in_=warm[:, 0:1], func=ACT.Sigmoid)
+        make_identity(nc, identity[:])
+
+        def x_rows(b, g):
+            rows = z[b, K_PASS * g : K_PASS * (g + 1)] if g < 2 else h[b]
+            return rows.rearrange("(p t) r c -> p t (r c)", t=PACK)
+
+        def m_rows(b):
+            return m[b].rearrange("(j p) r c -> p j (r c)", p=P)
+
+        def load_w_scales():
+            for quadrant in range(4):
+                nc.sync.dma_start(
+                    out=w_scales[32 * quadrant : 32 * quadrant + 4, :, :].bitcast(I32),
+                    in_=Wm_scales[:, 4 * quadrant : 4 * quadrant + 4, :]
+                    .rearrange("g r n -> r g n")
+                    .bitcast(I32),
+                )
+
+        first, second = slice(0, BLOCK), slice(BLOCK, PIXELS)
+        nc.sync.dma_start(out=bias_rows[0 : 3 * ROW_TILES, :], in_=bm.rearrange("(r c) -> r c", c=P))
+        for g in range(K_GROUPS):
+            nc.sync.dma_start(out=x_raw[0][g][:, :, first], in_=x_rows(0, g)[:, :, first])
+            if g == 0:
+                load_w_scales()
+            nc.sync.dma_start(out=w_words[:, g, :].bitcast(I32), in_=Wm_words[g].bitcast(I32))
+        nc.sync.dma_start(out=m_sb[0][:, :, first], in_=m_rows(0)[:, :, first])
+        for g in range(K_GROUPS):
+            nc.sync.dma_start(out=x_raw[0][g][:, :, second], in_=x_rows(0, g)[:, :, second])
+        nc.sync.dma_start(out=m_sb[0][:, :, second], in_=m_rows(0)[:, :, second])
+        for g in range(K_GROUPS):
+            nc.sync.dma_start(out=x_raw[1][g][:], in_=x_rows(1, g))
+        nc.sync.dma_start(out=m_sb[1][:], in_=m_rows(1))
+
+        bias_bank = psum.tile([P, P], BF16, tag="bank")
+        nc.tensor.transpose(bias_bank[:], bias_rows[:], identity[:])
+        nc.vector.tensor_copy(out=bias[:], in_=bias_bank[:, 0 : 3 * ROW_TILES])
+
+        def pixels_of(quarter):
+            half = quarter % HALVES
+            return quarter // HALVES, slice(BLOCK * half, BLOCK * (half + 1))
+
+        def quantise_piece(quarter, g, scalar_pixels):
+            b, cols = pixels_of(quarter)
+            grouped = group_pool.tile([P, BLOCK, PACK], BF16, align_bytes=64)
+            src = x_raw[b][g][:, :, cols].rearrange("p t (c i) -> p c t i", i=RUN)
+            dst = grouped[:].rearrange("p (c i) t -> p c t i", i=RUN)
+            cut = scalar_pixels // RUN
+            nc.scalar.copy(out=dst[:, :cut], in_=src[:, :cut])
+            nc.vector.tensor_copy(out=dst[:, cut:], in_=src[:, cut:])
+            piece = K_GROUPS * quarter + g
+            nc.vector.quantize_mx(
+                out=x_codes[:, piece, :].bitcast(FP8X4),
+                scales=x_scales[:, piece, :],
+                in_=grouped[:].rearrange("p w t -> p (w t)"),
+            )
+
+        def multiply(quarter, j, gate):
+            bank = psum.tile([P, BLOCK], F32, tag="bank")
+            tile_index = ROW_TILES * gate + j
+            for g in range(K_GROUPS):
+                piece = K_GROUPS * quarter + g
+                nc.tensor.matmul_mx(
+                    out=bank[:],
+                    lhsT=w_words[:, g, 2 * P * tile_index : 2 * P * (tile_index + 1)].bitcast(FP4X4),
+                    lhsT_scale=w_scales[:, g, P * tile_index : P * (tile_index + 1)],
+                    rhs=x_codes[:, piece, :].bitcast(FP8X4),
+                    rhs_scale=x_scales[:, piece, :],
+                    start=(g == 0),
+                    stop=(g == K_GROUPS - 1),
+                )
+            return bank
+
+        def activate(bank, j, gate, func, name):
+            result = gate_pool.tile([P, BLOCK], F32, name=name)
+            column = ROW_TILES * gate + j
+            nc.scalar.activation(
+                out=result[:], in_=bank[:], func=func, bias=bias[:, column : column + 1], scale=1.0
+            )
+            return result
+
+        for g in range(K_GROUPS):
+            quantise_piece(0, g, SCALAR_PIXELS_START)
+
+        live = {}
+        for unit in range(UNITS + 1):
+            if unit < UNITS:
+                quarter, j = divmod(unit, ROW_TILES)
+                b, cols = pixels_of(quarter)
+                bank_g = multiply(quarter, j, GATE_G)
+                bank_i = multiply(quarter, j, GATE_I)
+                bank_o = multiply(quarter, j, GATE_O)
+                tanh_g = activate(bank_g, j, GATE_G, ACT.Tanh, "tanh_g")
+                sig_i = activate(bank_i, j, GATE_I, ACT.Sigmoid, "sig_i")
+                sig_o = activate(bank_o, j, GATE_O, ACT.Sigmoid, "sig_o")
+                if quarter + 1 < QUARTERS and j < K_GROUPS:
+                    quantise_piece(quarter + 1, j, SCALAR_PIXELS)
+                step = gate_pool.tile([P, BLOCK], F32, name="step")
+                nc.vector.tensor_tensor(
+                    out=step[:], in0=tanh_g[:], in1=m_sb[b][:, j, cols], op=ALU.subtract
+                )
+            if unit > 0:
+                old = live[unit - 1]
+                new_m = gate_pool.tile([P, BLOCK], F32, name="new_m")
+                nc.vector.tensor_tensor(out=new_m[:], in0=old["step"][:], in1=old["m"], op=ALU.add)
+                nc.sync.dma_start(out=old["out_m"], in_=new_m[:])
+            if unit < UNITS:
+                nc.vector.tensor_tensor(out=step[:], in0=step[:], in1=sig_i[:], op=ALU.mult)
+                rows = slice(P * j, P * (j + 1))
+                live[unit] = {
+                    "step": step,
+                    "m": m_sb[b][:, j, cols],
+                    "sig_o": sig_o,
+                    "out_h": out_0[b, rows].rearrange("p r c -> p (r c)")[:, cols],
+                    "out_m": out_1[b, rows].rearrange("p r c -> p (r c)")[:, cols],
+                }
+            if unit > 0:
+                new_h = gate_pool.tile([P, BLOCK], F32, name="new_h")
+                nc.vector.tensor_tensor(out=new_h[:], in0=new_m[:], in1=old["sig_o"][:], op=ALU.mult)
+                nc.sync.dma_start(out=old["out_h"], in_=new_h[:])

@@ -43,6 +43,7 @@ def tile_self_attention_memory_module_pb_kernel(
         group_pool = ctx.enter_context(tc.tile_pool(name="group", bufs=3))
         gate_pool = ctx.enter_context(tc.tile_pool(name="gate", bufs=4))
         psum = ctx.enter_context(tc.psum_pool(name="psum", bufs=8))
+        ctx.enter_context(tc.manual_schedule())
 
         x_raw = [
             [keep.tile([P, PACK, PIXELS], BF16, name="x_raw_%d_%d" % (b, g)) for g in range(K_GROUPS)]
@@ -103,7 +104,7 @@ def tile_self_attention_memory_module_pb_kernel(
             half = quarter % HALVES
             return quarter // HALVES, slice(BLOCK * half, BLOCK * (half + 1))
 
-        def quantise_piece(quarter, g, scalar_pixels):
+        def regroup_piece(quarter, g, scalar_pixels):
             b, cols = pixels_of(quarter)
             grouped = group_pool.tile([P, BLOCK, PACK], BF16, align_bytes=64)
             src = x_raw[b][g][:, :, cols].rearrange("p t (c i) -> p c t i", i=RUN)
@@ -111,7 +112,9 @@ def tile_self_attention_memory_module_pb_kernel(
             cut = scalar_pixels // RUN
             nc.scalar.copy(out=dst[:, :cut], in_=src[:, :cut])
             nc.vector.tensor_copy(out=dst[:, cut:], in_=src[:, cut:])
-            piece = K_GROUPS * quarter + g
+            return grouped, K_GROUPS * quarter + g
+
+        def quantise_piece(grouped, piece):
             nc.vector.quantize_mx(
                 out=x_codes[:, piece, :].bitcast(FP8X4),
                 scales=x_scales[:, piece, :],
@@ -143,9 +146,11 @@ def tile_self_attention_memory_module_pb_kernel(
             return result
 
         for g in range(K_GROUPS):
-            quantise_piece(0, g, SCALAR_PIXELS_START)
+            grouped, piece = regroup_piece(0, g, SCALAR_PIXELS_START)
+            quantise_piece(grouped, piece)
 
         live = {}
+        copied = None
         for unit in range(UNITS + 1):
             if unit < UNITS:
                 quarter, j = divmod(unit, ROW_TILES)
@@ -156,8 +161,10 @@ def tile_self_attention_memory_module_pb_kernel(
                 tanh_g = activate(bank_g, j, GATE_G, ACT.Tanh, "tanh_g")
                 sig_i = activate(bank_i, j, GATE_I, ACT.Sigmoid, "sig_i")
                 sig_o = activate(bank_o, j, GATE_O, ACT.Sigmoid, "sig_o")
-                if quarter + 1 < QUARTERS and j < K_GROUPS:
-                    quantise_piece(quarter + 1, j, SCALAR_PIXELS)
+            if copied is not None:
+                quantise_piece(copied[0], copied[1])
+                copied = None
+            if unit < UNITS:
                 step = gate_pool.tile([P, BLOCK], F32, name="step")
                 nc.vector.tensor_tensor(
                     out=step[:], in0=tanh_g[:], in1=m_sb[b][:, j, cols], op=ALU.subtract
@@ -168,6 +175,8 @@ def tile_self_attention_memory_module_pb_kernel(
                 nc.vector.tensor_tensor(out=new_m[:], in0=old["step"][:], in1=old["m"], op=ALU.add)
                 nc.sync.dma_start(out=old["out_m"], in_=new_m[:])
             if unit < UNITS:
+                if quarter + 1 < QUARTERS and j < K_GROUPS:
+                    copied = regroup_piece(quarter + 1, j, SCALAR_PIXELS)
                 nc.vector.tensor_tensor(out=step[:], in0=step[:], in1=sig_i[:], op=ALU.mult)
                 rows = slice(P * j, P * (j + 1))
                 live[unit] = {

@@ -43,13 +43,7 @@ def tile_self_attention_memory_module_pb_kernel(
         group_pool = ctx.enter_context(tc.tile_pool(name="group", bufs=3))
         gate_pool = ctx.enter_context(tc.tile_pool(name="gate", bufs=4))
         psum = ctx.enter_context(tc.psum_pool(name="psum", bufs=8))
-        ctx.enter_context(tc.manual_schedule())
 
-        x_raw = [
-            [keep.tile([P, PACK, PIXELS], BF16, name="x_raw_%d_%d" % (b, g)) for g in range(K_GROUPS)]
-            for b in range(BATCH)
-        ]
-        m_sb = [keep.tile([P, ROW_TILES, PIXELS], BF16, name="m_sb_%d" % b) for b in range(BATCH)]
         x_codes = keep.tile([P, QUARTERS * K_GROUPS, BLOCK], U32, align_bytes=64)
         x_scales = keep.tile([P, QUARTERS * K_GROUPS, BLOCK], U8, align_bytes=64)
         w_words = keep.tile([P, K_GROUPS, 2 * 3 * C], U8, align_bytes=64)
@@ -59,11 +53,15 @@ def tile_self_attention_memory_module_pb_kernel(
         bias = keep.tile([P, 3 * ROW_TILES], F32)
         warm = keep.tile([P, 2], F32)
 
-        nc.vector.memset(w_scales[:].bitcast(I32), 0)
         nc.vector.memset(bias_rows[:], 0.0)
         nc.vector.memset(warm[:, 0:1], 0.0)
+        nc.vector.memset(w_scales[:].bitcast(I32), 0)
         nc.scalar.activation(out=warm[:, 1:2], in_=warm[:, 0:1], func=ACT.Sigmoid)
         make_identity(nc, identity[:])
+
+        def pixels_of(quarter):
+            half = quarter % HALVES
+            return quarter // HALVES, slice(BLOCK * half, BLOCK * (half + 1))
 
         def x_rows(b, g):
             rows = z[b, K_PASS * g : K_PASS * (g + 1)] if g < 2 else h[b]
@@ -81,33 +79,48 @@ def tile_self_attention_memory_module_pb_kernel(
                     .bitcast(I32),
                 )
 
-        first, second = slice(0, BLOCK), slice(BLOCK, PIXELS)
-        nc.sync.dma_start(out=bias_rows[0 : 3 * ROW_TILES, :], in_=bm.rearrange("(r c) -> r c", c=P))
+        x_piece = {}
+        m_block = {}
+
+        def load_x_block(quarter, g):
+            b, cols = pixels_of(quarter)
+            x_piece[quarter, g] = keep.tile([P, PACK, BLOCK], BF16, name="x_%d_%d" % (quarter, g))
+            nc.sync.dma_start(out=x_piece[quarter, g][:], in_=x_rows(b, g)[:, :, cols])
+
+        def load_m_block(quarter):
+            b, cols = pixels_of(quarter)
+            m_block[quarter] = keep.tile([P, ROW_TILES, BLOCK], BF16, name="m_%d" % quarter)
+            nc.sync.dma_start(out=m_block[quarter][:], in_=m_rows(b)[:, :, cols])
+
         for g in range(K_GROUPS):
-            nc.sync.dma_start(out=x_raw[0][g][:, :, first], in_=x_rows(0, g)[:, :, first])
+            load_x_block(0, g)
             if g == 0:
+                nc.sync.dma_start(
+                    out=bias_rows[0 : 3 * ROW_TILES, :], in_=bm.rearrange("(r c) -> r c", c=P)
+                )
                 load_w_scales()
             nc.sync.dma_start(out=w_words[:, g, :].bitcast(I32), in_=Wm_words[g].bitcast(I32))
-        nc.sync.dma_start(out=m_sb[0][:, :, first], in_=m_rows(0)[:, :, first])
+        load_m_block(0)
         for g in range(K_GROUPS):
-            nc.sync.dma_start(out=x_raw[0][g][:, :, second], in_=x_rows(0, g)[:, :, second])
-        nc.sync.dma_start(out=m_sb[0][:, :, second], in_=m_rows(0)[:, :, second])
+            load_x_block(1, g)
+        load_m_block(1)
         for g in range(K_GROUPS):
-            nc.sync.dma_start(out=x_raw[1][g][:], in_=x_rows(1, g))
-        nc.sync.dma_start(out=m_sb[1][:], in_=m_rows(1))
+            x_whole = keep.tile([P, PACK, PIXELS], BF16, name="x_whole_%d" % g)
+            nc.sync.dma_start(out=x_whole[:], in_=x_rows(1, g))
+            for quarter in range(HALVES, QUARTERS):
+                x_piece[quarter, g] = x_whole[:, :, pixels_of(quarter)[1]]
+        m_whole = keep.tile([P, ROW_TILES, PIXELS], BF16)
+        nc.sync.dma_start(out=m_whole[:], in_=m_rows(1))
+        for quarter in range(HALVES, QUARTERS):
+            m_block[quarter] = m_whole[:, :, pixels_of(quarter)[1]]
 
         bias_bank = psum.tile([P, P], BF16, tag="bank")
         nc.tensor.transpose(bias_bank[:], bias_rows[:], identity[:])
         nc.vector.tensor_copy(out=bias[:], in_=bias_bank[:, 0 : 3 * ROW_TILES])
 
-        def pixels_of(quarter):
-            half = quarter % HALVES
-            return quarter // HALVES, slice(BLOCK * half, BLOCK * (half + 1))
-
         def regroup_piece(quarter, g, scalar_pixels):
-            b, cols = pixels_of(quarter)
             grouped = group_pool.tile([P, BLOCK, PACK], BF16, align_bytes=64)
-            src = x_raw[b][g][:, :, cols].rearrange("p t (c i) -> p c t i", i=RUN)
+            src = x_piece[quarter, g].rearrange("p t (c i) -> p c t i", i=RUN)
             dst = grouped[:].rearrange("p (c i) t -> p c t i", i=RUN)
             cut = scalar_pixels // RUN
             nc.scalar.copy(out=dst[:, :cut], in_=src[:, :cut])
@@ -167,7 +180,7 @@ def tile_self_attention_memory_module_pb_kernel(
             if unit < UNITS:
                 step = gate_pool.tile([P, BLOCK], F32, name="step")
                 nc.vector.tensor_tensor(
-                    out=step[:], in0=tanh_g[:], in1=m_sb[b][:, j, cols], op=ALU.subtract
+                    out=step[:], in0=tanh_g[:], in1=m_block[quarter][:, j, :], op=ALU.subtract
                 )
             if unit > 0:
                 old = live[unit - 1]
@@ -181,7 +194,7 @@ def tile_self_attention_memory_module_pb_kernel(
                 rows = slice(P * j, P * (j + 1))
                 live[unit] = {
                     "step": step,
-                    "m": m_sb[b][:, j, cols],
+                    "m": m_block[quarter][:, j, :],
                     "sig_o": sig_o,
                     "out_h": out_0[b, rows].rearrange("p r c -> p (r c)")[:, cols],
                     "out_m": out_1[b, rows].rearrange("p r c -> p (r c)")[:, cols],

@@ -29,7 +29,7 @@ GATE_O, GATE_G, GATE_I = 0, 1, 2
 RUN = 4
 
 SCALAR_PIXELS_START = 176
-SCALAR_PIXELS = 384
+SCALAR_PIXELS = 320
 
 FLOPS = 2 * (3 * C) * (3 * C) * BATCH * PIXELS
 
@@ -170,6 +170,10 @@ def tile_self_attention_memory_module_pb_kernel(
                 b, cols = pixels_of(quarter)
                 bank_g = multiply(quarter, j, GATE_G)
                 bank_i = multiply(quarter, j, GATE_I)
+                m_bank = psum.tile([P, BLOCK], F32, tag="bank")
+                nc.tensor.matmul(
+                    out=m_bank[:], lhsT=identity[:], rhs=m_block[quarter][:, j, :], start=True, stop=True
+                )
                 bank_o = multiply(quarter, j, GATE_O)
                 tanh_g = activate(bank_g, j, GATE_G, ACT.Tanh, "tanh_g")
                 sig_i = activate(bank_i, j, GATE_I, ACT.Sigmoid, "sig_i")
@@ -179,13 +183,11 @@ def tile_self_attention_memory_module_pb_kernel(
                 copied = None
             if unit < UNITS:
                 step = gate_pool.tile([P, BLOCK], F32, name="step")
-                nc.vector.tensor_tensor(
-                    out=step[:], in0=tanh_g[:], in1=m_block[quarter][:, j, :], op=ALU.subtract
-                )
+                nc.vector.tensor_tensor(out=step[:], in0=tanh_g[:], in1=m_bank[:], op=ALU.subtract)
             if unit > 0:
                 old = live[unit - 1]
                 new_m = gate_pool.tile([P, BLOCK], F32, name="new_m")
-                nc.vector.tensor_tensor(out=new_m[:], in0=old["step"][:], in1=old["m"], op=ALU.add)
+                nc.vector.tensor_tensor(out=new_m[:], in0=old["step"][:], in1=old["m"][:], op=ALU.add)
                 nc.sync.dma_start(out=old["out_m"], in_=new_m[:])
             if unit < UNITS:
                 if quarter + 1 < QUARTERS and j < K_GROUPS:
@@ -194,12 +196,12 @@ def tile_self_attention_memory_module_pb_kernel(
                 rows = slice(P * j, P * (j + 1))
                 live[unit] = {
                     "step": step,
-                    "m": m_block[quarter][:, j, :],
+                    "m": m_bank,
                     "sig_o": sig_o,
                     "out_h": out_0[b, rows].rearrange("p r c -> p (r c)")[:, cols],
                     "out_m": out_1[b, rows].rearrange("p r c -> p (r c)")[:, cols],
                 }
             if unit > 0:
                 new_h = gate_pool.tile([P, BLOCK], F32, name="new_h")
-                nc.vector.tensor_tensor(out=new_h[:], in0=new_m[:], in1=old["sig_o"][:], op=ALU.mult)
+                nc.gpsimd.tensor_tensor(out=new_h[:], in0=new_m[:], in1=old["sig_o"][:], op=ALU.mult)
                 nc.sync.dma_start(out=old["out_h"], in_=new_h[:])

@@ -28,8 +28,7 @@ UNITS = QUARTERS * ROW_TILES
 GATE_O, GATE_G, GATE_I = 0, 1, 2
 RUN = 4
 
-SCALAR_PIXELS_START = 176
-SCALAR_PIXELS = 320
+VECTOR_PIECES = 1
 
 FLOPS = 2 * (3 * C) * (3 * C) * BATCH * PIXELS
 
@@ -118,13 +117,14 @@ def tile_self_attention_memory_module_pb_kernel(
         nc.tensor.transpose(bias_bank[:], bias_rows[:], identity[:])
         nc.vector.tensor_copy(out=bias[:], in_=bias_bank[:, 0 : 3 * ROW_TILES])
 
-        def regroup_piece(quarter, g, scalar_pixels):
+        def regroup_piece(quarter, g):
             grouped = group_pool.tile([P, BLOCK, PACK], BF16, align_bytes=64)
             src = x_piece[quarter, g].rearrange("p t (c i) -> p c t i", i=RUN)
             dst = grouped[:].rearrange("p (c i) t -> p c t i", i=RUN)
-            cut = scalar_pixels // RUN
-            nc.scalar.copy(out=dst[:, :cut], in_=src[:, :cut])
-            nc.vector.tensor_copy(out=dst[:, cut:], in_=src[:, cut:])
+            if g < VECTOR_PIECES or (quarter == 0 and g == K_GROUPS - 1):
+                nc.vector.tensor_copy(out=dst, in_=src)
+            else:
+                nc.scalar.copy(out=dst, in_=src)
             return grouped, K_GROUPS * quarter + g
 
         def quantise_piece(grouped, piece):
@@ -159,7 +159,7 @@ def tile_self_attention_memory_module_pb_kernel(
             return result
 
         for g in range(K_GROUPS):
-            grouped, piece = regroup_piece(0, g, SCALAR_PIXELS_START)
+            grouped, piece = regroup_piece(0, g)
             quantise_piece(grouped, piece)
 
         live = {}
@@ -170,10 +170,6 @@ def tile_self_attention_memory_module_pb_kernel(
                 b, cols = pixels_of(quarter)
                 bank_g = multiply(quarter, j, GATE_G)
                 bank_i = multiply(quarter, j, GATE_I)
-                m_bank = psum.tile([P, BLOCK], F32, tag="bank")
-                nc.tensor.matmul(
-                    out=m_bank[:], lhsT=identity[:], rhs=m_block[quarter][:, j, :], start=True, stop=True
-                )
                 bank_o = multiply(quarter, j, GATE_O)
                 tanh_g = activate(bank_g, j, GATE_G, ACT.Tanh, "tanh_g")
                 sig_i = activate(bank_i, j, GATE_I, ACT.Sigmoid, "sig_i")
@@ -183,25 +179,27 @@ def tile_self_attention_memory_module_pb_kernel(
                 copied = None
             if unit < UNITS:
                 step = gate_pool.tile([P, BLOCK], F32, name="step")
-                nc.vector.tensor_tensor(out=step[:], in0=tanh_g[:], in1=m_bank[:], op=ALU.subtract)
+                nc.vector.tensor_tensor(
+                    out=step[:], in0=tanh_g[:], in1=m_block[quarter][:, j, :], op=ALU.subtract
+                )
             if unit > 0:
                 old = live[unit - 1]
                 new_m = gate_pool.tile([P, BLOCK], F32, name="new_m")
-                nc.vector.tensor_tensor(out=new_m[:], in0=old["step"][:], in1=old["m"][:], op=ALU.add)
+                nc.vector.tensor_tensor(out=new_m[:], in0=old["step"][:], in1=old["m"], op=ALU.add)
                 nc.sync.dma_start(out=old["out_m"], in_=new_m[:])
             if unit < UNITS:
                 if quarter + 1 < QUARTERS and j < K_GROUPS:
-                    copied = regroup_piece(quarter + 1, j, SCALAR_PIXELS)
+                    copied = regroup_piece(quarter + 1, j)
                 nc.vector.tensor_tensor(out=step[:], in0=step[:], in1=sig_i[:], op=ALU.mult)
                 rows = slice(P * j, P * (j + 1))
                 live[unit] = {
                     "step": step,
-                    "m": m_bank,
+                    "m": m_block[quarter][:, j, :],
                     "sig_o": sig_o,
                     "out_h": out_0[b, rows].rearrange("p r c -> p (r c)")[:, cols],
                     "out_m": out_1[b, rows].rearrange("p r c -> p (r c)")[:, cols],
                 }
             if unit > 0:
                 new_h = gate_pool.tile([P, BLOCK], F32, name="new_h")
-                nc.gpsimd.tensor_tensor(out=new_h[:], in0=new_m[:], in1=old["sig_o"][:], op=ALU.mult)
+                nc.vector.tensor_tensor(out=new_h[:], in0=new_m[:], in1=old["sig_o"][:], op=ALU.mult)
                 nc.sync.dma_start(out=old["out_h"], in_=new_h[:])

@@ -26,9 +26,14 @@ QUARTERS = BATCH * HALVES
 ROW_TILES = C // P
 UNITS = QUARTERS * ROW_TILES
 GATE_O, GATE_G, GATE_I = 0, 1, 2
+GATES = 3
+W_HALVES = 2
+TILES_PER_HALF = ROW_TILES // W_HALVES
 RUN = 4
 
 VECTOR_PIECES = 1
+WARM_PASSES = 7
+HEAD_VECTOR_PIXELS = 320
 
 FLOPS = 2 * (3 * C) * (3 * C) * BATCH * PIXELS
 
@@ -45,7 +50,7 @@ def tile_self_attention_memory_module_pb_kernel(
 
         x_codes = keep.tile([P, QUARTERS * K_GROUPS, BLOCK], U32, align_bytes=64)
         x_scales = keep.tile([P, QUARTERS * K_GROUPS, BLOCK], U8, align_bytes=64)
-        w_words = keep.tile([P, K_GROUPS, 2 * 3 * C], U8, align_bytes=64)
+        w_words = {}
         w_scales = keep.tile([P, K_GROUPS, 3 * C], U8, align_bytes=64)
         bias_rows = keep.tile([P, P], BF16)
         identity = keep.tile([P, P], BF16)
@@ -57,6 +62,11 @@ def tile_self_attention_memory_module_pb_kernel(
         nc.vector.memset(w_scales[:].bitcast(I32), 0)
         nc.scalar.activation(out=warm[:, 1:2], in_=warm[:, 0:1], func=ACT.Sigmoid)
         make_identity(nc, identity[:])
+        zeros = keep.tile([P, BLOCK], BF16)
+        nc.gpsimd.memset(zeros[:], 0.0)
+        warm_bank = psum.tile([P, BLOCK], F32, tag="bank")
+        for i in range(WARM_PASSES):
+            nc.tensor.matmul(out=warm_bank[:], lhsT=identity[:], rhs=zeros[:], start=True, stop=True)
 
         def pixels_of(quarter):
             half = quarter % HALVES
@@ -91,6 +101,18 @@ def tile_self_attention_memory_module_pb_kernel(
             m_block[quarter] = keep.tile([P, ROW_TILES, BLOCK], BF16, name="m_%d" % quarter)
             nc.sync.dma_start(out=m_block[quarter][:], in_=m_rows(b)[:, :, cols])
 
+        def load_w_words(half, g):
+            nc.sync.dma_start(
+                out=w_words[half][:, g, :, :].bitcast(I32),
+                in_=Wm_words[g]
+                .rearrange("p (a h c) -> p a h c", a=GATES, h=W_HALVES)[:, :, half, :]
+                .bitcast(I32),
+            )
+
+        for half in range(W_HALVES):
+            w_words[half] = keep.tile(
+                [P, K_GROUPS, GATES, 2 * C // W_HALVES], U8, align_bytes=64, name="w_words_%d" % half
+            )
         for g in range(K_GROUPS):
             load_x_block(0, g)
             if g == 0:
@@ -98,9 +120,12 @@ def tile_self_attention_memory_module_pb_kernel(
                     out=bias_rows[0 : 3 * ROW_TILES, :], in_=bm.rearrange("(r c) -> r c", c=P)
                 )
                 load_w_scales()
-            nc.sync.dma_start(out=w_words[:, g, :].bitcast(I32), in_=Wm_words[g].bitcast(I32))
+            load_w_words(0, g)
         load_m_block(0)
+        load_x_block(1, 0)
         for g in range(K_GROUPS):
+            load_w_words(1, g)
+        for g in range(1, K_GROUPS):
             load_x_block(1, g)
         load_m_block(1)
         for g in range(K_GROUPS):
@@ -121,7 +146,11 @@ def tile_self_attention_memory_module_pb_kernel(
             grouped = group_pool.tile([P, BLOCK, PACK], BF16, align_bytes=64)
             src = x_piece[quarter, g].rearrange("p t (c i) -> p c t i", i=RUN)
             dst = grouped[:].rearrange("p (c i) t -> p c t i", i=RUN)
-            if g < VECTOR_PIECES or (quarter == 0 and g == K_GROUPS - 1):
+            if quarter == 0:
+                cut = HEAD_VECTOR_PIXELS // RUN
+                nc.vector.tensor_copy(out=dst[:, 0:cut], in_=src[:, 0:cut])
+                nc.scalar.copy(out=dst[:, cut:], in_=src[:, cut:])
+            elif g < VECTOR_PIECES:
                 nc.vector.tensor_copy(out=dst, in_=src)
             else:
                 nc.scalar.copy(out=dst, in_=src)
@@ -141,7 +170,9 @@ def tile_self_attention_memory_module_pb_kernel(
                 piece = K_GROUPS * quarter + g
                 nc.tensor.matmul_mx(
                     out=bank[:],
-                    lhsT=w_words[:, g, 2 * P * tile_index : 2 * P * (tile_index + 1)].bitcast(FP4X4),
+                    lhsT=w_words[j // TILES_PER_HALF][
+                        :, g, gate, 2 * P * (j % TILES_PER_HALF) : 2 * P * (j % TILES_PER_HALF + 1)
+                    ].bitcast(FP4X4),
                     lhsT_scale=w_scales[:, g, P * tile_index : P * (tile_index + 1)],
                     rhs=x_codes[:, piece, :].bitcast(FP8X4),
                     rhs_scale=x_scales[:, piece, :],

@@ -32,6 +32,9 @@ TILES_PER_HALF = ROW_TILES // W_HALVES
 RUN = 4
 
 VECTOR_PIECES = 1
+VECTOR_IN_ROUND = {0: (1, 0), 1: (1, 1), 2: (2, 0)}
+SCALAR_FROM_ROUND = {2: (1, 2), 3: (3, 0), 5: (2, 1), 6: (2, 2), 9: (3, 1), 10: (3, 2)}
+SCALAR_CHUNKS = 4
 WARM_PASSES = 7
 HEAD_VECTOR_PIXELS = 320
 
@@ -44,7 +47,7 @@ def tile_self_attention_memory_module_pb_kernel(
     nc = tc.nc
     with ExitStack() as ctx:
         keep = ctx.enter_context(tc.tile_pool(name="keep", bufs=1))
-        group_pool = ctx.enter_context(tc.tile_pool(name="group", bufs=3))
+        group_pool = ctx.enter_context(tc.tile_pool(name="group", bufs=5))
         gate_pool = ctx.enter_context(tc.tile_pool(name="gate", bufs=4))
         psum = ctx.enter_context(tc.psum_pool(name="psum", bufs=8))
 
@@ -143,17 +146,15 @@ def tile_self_attention_memory_module_pb_kernel(
         nc.vector.tensor_copy(out=bias[:], in_=bias_bank[:, 0 : 3 * ROW_TILES])
 
         def regroup_piece(quarter, g):
-            grouped = group_pool.tile([P, BLOCK, PACK], BF16, align_bytes=64)
+            grouped = group_pool.tile([P, BLOCK, PACK], BF16, align_bytes=64, name="grouped")
             src = x_piece[quarter, g].rearrange("p t (c i) -> p c t i", i=RUN)
             dst = grouped[:].rearrange("p (c i) t -> p c t i", i=RUN)
             if quarter == 0:
                 cut = HEAD_VECTOR_PIXELS // RUN
                 nc.vector.tensor_copy(out=dst[:, 0:cut], in_=src[:, 0:cut])
                 nc.scalar.copy(out=dst[:, cut:], in_=src[:, cut:])
-            elif g < VECTOR_PIECES:
-                nc.vector.tensor_copy(out=dst, in_=src)
             else:
-                nc.scalar.copy(out=dst, in_=src)
+                nc.vector.tensor_copy(out=dst, in_=src)
             return grouped, K_GROUPS * quarter + g
 
         def quantise_piece(grouped, piece):
@@ -181,12 +182,30 @@ def tile_self_attention_memory_module_pb_kernel(
                 )
             return bank
 
+        scalar_chunks = []
+        progress = {"chunks": 0}
+        copied = []
+
+        def next_scalar_chunk():
+            if progress["chunks"] == len(scalar_chunks):
+                return
+            grouped, quarter, g, c = scalar_chunks[progress["chunks"]]
+            progress["chunks"] += 1
+            part = slice(c * BLOCK // SCALAR_CHUNKS, (c + 1) * BLOCK // SCALAR_CHUNKS)
+            nc.scalar.copy(
+                out=grouped[:, part, :].rearrange("p (c i) t -> p c t i", i=RUN),
+                in_=x_piece[quarter, g][:, :, part].rearrange("p t (c i) -> p c t i", i=RUN),
+            )
+            if c == SCALAR_CHUNKS - 1:
+                copied.append((grouped, K_GROUPS * quarter + g))
+
         def activate(bank, j, gate, func, name):
             result = gate_pool.tile([P, BLOCK], F32, name=name)
             column = ROW_TILES * gate + j
             nc.scalar.activation(
                 out=result[:], in_=bank[:], func=func, bias=bias[:, column : column + 1], scale=1.0
             )
+            next_scalar_chunk()
             return result
 
         for g in range(K_GROUPS):
@@ -194,20 +213,23 @@ def tile_self_attention_memory_module_pb_kernel(
             quantise_piece(grouped, piece)
 
         live = {}
-        copied = None
         for unit in range(UNITS + 1):
             if unit < UNITS:
                 quarter, j = divmod(unit, ROW_TILES)
                 b, cols = pixels_of(quarter)
+                if unit in SCALAR_FROM_ROUND:
+                    grouped = group_pool.tile([P, BLOCK, PACK], BF16, align_bytes=64, name="grouped")
+                    for c in range(SCALAR_CHUNKS):
+                        scalar_chunks.append((grouped,) + SCALAR_FROM_ROUND[unit] + (c,))
                 bank_g = multiply(quarter, j, GATE_G)
                 bank_i = multiply(quarter, j, GATE_I)
                 bank_o = multiply(quarter, j, GATE_O)
                 tanh_g = activate(bank_g, j, GATE_G, ACT.Tanh, "tanh_g")
                 sig_i = activate(bank_i, j, GATE_I, ACT.Sigmoid, "sig_i")
                 sig_o = activate(bank_o, j, GATE_O, ACT.Sigmoid, "sig_o")
-            if copied is not None:
-                quantise_piece(copied[0], copied[1])
-                copied = None
+            for grouped, piece in copied:
+                quantise_piece(grouped, piece)
+            copied.clear()
             if unit < UNITS:
                 step = gate_pool.tile([P, BLOCK], F32, name="step")
                 nc.vector.tensor_tensor(
@@ -219,8 +241,8 @@ def tile_self_attention_memory_module_pb_kernel(
                 nc.vector.tensor_tensor(out=new_m[:], in0=old["step"][:], in1=old["m"], op=ALU.add)
                 nc.sync.dma_start(out=old["out_m"], in_=new_m[:])
             if unit < UNITS:
-                if quarter + 1 < QUARTERS and j < K_GROUPS:
-                    copied = regroup_piece(quarter + 1, j)
+                if unit in VECTOR_IN_ROUND:
+                    copied.append(regroup_piece(VECTOR_IN_ROUND[unit][0], VECTOR_IN_ROUND[unit][1]))
                 nc.vector.tensor_tensor(out=step[:], in0=step[:], in1=sig_i[:], op=ALU.mult)
                 rows = slice(P * j, P * (j + 1))
                 live[unit] = {

@@ -32,6 +32,7 @@ TILES_PER_HALF = ROW_TILES // W_HALVES
 RUN = 4
 
 VECTOR_PIECES = 1
+LAST_PARTS = 2
 VECTOR_IN_ROUND = {0: (1, 0), 1: (1, 1), 2: (2, 0)}
 SCALAR_FROM_ROUND = {2: (1, 2), 3: (3, 0), 5: (2, 1), 6: (2, 2), 9: (3, 1), 10: (3, 2)}
 SCALAR_CHUNKS = 4
@@ -254,5 +255,10 @@ def tile_self_attention_memory_module_pb_kernel(
                 }
             if unit > 0:
                 new_h = gate_pool.tile([P, BLOCK], F32, name="new_h")
-                nc.vector.tensor_tensor(out=new_h[:], in0=new_m[:], in1=old["sig_o"][:], op=ALU.mult)
-                nc.sync.dma_start(out=old["out_h"], in_=new_h[:])
+                parts = LAST_PARTS if unit == UNITS else 1
+                for part in range(parts):
+                    some = slice(part * BLOCK // parts, (part + 1) * BLOCK // parts)
+                    nc.vector.tensor_tensor(
+                        out=new_h[:, some], in0=new_m[:, some], in1=old["sig_o"][:, some], op=ALU.mult
+                    )
+                    nc.sync.dma_start(out=old["out_h"][:, some], in_=new_h[:, some])

@@ -35,7 +35,7 @@ VECTOR_PIECES = 1
 LAST_PARTS = 2
 VECTOR_IN_ROUND = {0: (1, 0), 1: (1, 1), 2: (2, 0)}
 SCALAR_FROM_ROUND = {2: (1, 2), 3: (3, 0), 5: (2, 1), 6: (2, 2), 9: (3, 1), 10: (3, 2)}
-SCALAR_CHUNKS = 4
+SCALAR_CHUNKS = 2
 WARM_PASSES = 7
 HEAD_VECTOR_PIXELS = 320
 

@@ -35,7 +35,7 @@ VECTOR_PIECES = 1
 LAST_PARTS = 2
 VECTOR_IN_ROUND = {0: (1, 0), 1: (1, 1), 2: (2, 0)}
 SCALAR_FROM_ROUND = {2: (1, 2), 3: (3, 0), 5: (2, 1), 6: (2, 2), 9: (3, 1), 10: (3, 2)}
-SCALAR_CHUNKS = 2
+SCALAR_CHUNKS = 1
 WARM_PASSES = 7
 HEAD_VECTOR_PIXELS = 320
 

from contextlib import ExitStack

import concourse.mybir as mybir
from concourse.masks import make_identity

BF16 = mybir.dt.bfloat16
F32 = mybir.dt.float32
I32 = mybir.dt.int32
U8 = mybir.dt.uint8
U32 = mybir.dt.uint32
FP8X4 = mybir.dt.float8_e4m3fn_x4
FP4X4 = mybir.dt.float4_e2m1fn_x4
ACT = mybir.ActivationFunctionType
ALU = mybir.AluOpType

P = 128
PACK = 4
K_PASS = P * PACK
BATCH = 2
C = 512
PIXELS = 1024
K_GROUPS = 3
BLOCK = 512
HALVES = PIXELS // BLOCK
QUARTERS = BATCH * HALVES
ROW_TILES = C // P
UNITS = QUARTERS * ROW_TILES
GATE_O, GATE_G, GATE_I = 0, 1, 2
GATES = 3
W_HALVES = 2
TILES_PER_HALF = ROW_TILES // W_HALVES
RUN = 4

VECTOR_PIECES = 1
LAST_PARTS = 2
VECTOR_IN_ROUND = {0: (1, 0), 1: (1, 1), 2: (2, 0)}
SCALAR_FROM_ROUND = {2: (1, 2), 3: (3, 0), 5: (2, 1), 6: (2, 2), 9: (3, 1), 10: (3, 2)}
SCALAR_CHUNKS = 1
WARM_PASSES = 7
HEAD_VECTOR_PIXELS = 320

FLOPS = 2 * (3 * C) * (3 * C) * BATCH * PIXELS


def tile_self_attention_memory_module_pb_kernel(
    tc, z, h, m, Wm_words, Wm_scales, bm, out_0, out_1
):
    nc = tc.nc
    with ExitStack() as ctx:
        keep = ctx.enter_context(tc.tile_pool(name="keep", bufs=1))
        group_pool = ctx.enter_context(tc.tile_pool(name="group", bufs=5))
        gate_pool = ctx.enter_context(tc.tile_pool(name="gate", bufs=4))
        psum = ctx.enter_context(tc.psum_pool(name="psum", bufs=8))

        x_codes = keep.tile([P, QUARTERS * K_GROUPS, BLOCK], U32, align_bytes=64)
        x_scales = keep.tile([P, QUARTERS * K_GROUPS, BLOCK], U8, align_bytes=64)
        w_words = {}
        w_scales = keep.tile([P, K_GROUPS, 3 * C], U8, align_bytes=64)
        bias_rows = keep.tile([P, P], BF16)
        identity = keep.tile([P, P], BF16)
        bias = keep.tile([P, 3 * ROW_TILES], F32)
        warm = keep.tile([P, 2], F32)

        nc.vector.memset(bias_rows[:], 0.0)
        nc.vector.memset(warm[:, 0:1], 0.0)
        nc.vector.memset(w_scales[:].bitcast(I32), 0)
        nc.scalar.activation(out=warm[:, 1:2], in_=warm[:, 0:1], func=ACT.Sigmoid)
        make_identity(nc, identity[:])
        zeros = keep.tile([P, BLOCK], BF16)
        nc.gpsimd.memset(zeros[:], 0.0)
        warm_bank = psum.tile([P, BLOCK], F32, tag="bank")
        for i in range(WARM_PASSES):
            nc.tensor.matmul(out=warm_bank[:], lhsT=identity[:], rhs=zeros[:], start=True, stop=True)

        def pixels_of(quarter):
            half = quarter % HALVES
            return quarter // HALVES, slice(BLOCK * half, BLOCK * (half + 1))

        def x_rows(b, g):
            rows = z[b, K_PASS * g : K_PASS * (g + 1)] if g < 2 else h[b]
            return rows.rearrange("(p t) r c -> p t (r c)", t=PACK)

        def m_rows(b):
            return m[b].rearrange("(j p) r c -> p j (r c)", p=P)

        def load_w_scales():
            for quadrant in range(4):
                nc.sync.dma_start(
                    out=w_scales[32 * quadrant : 32 * quadrant + 4, :, :].bitcast(I32),
                    in_=Wm_scales[:, 4 * quadrant : 4 * quadrant + 4, :]
                    .rearrange("g r n -> r g n")
                    .bitcast(I32),
                )

        x_piece = {}
        m_block = {}

        def load_x_block(quarter, g):
            b, cols = pixels_of(quarter)
            x_piece[quarter, g] = keep.tile([P, PACK, BLOCK], BF16, name="x_%d_%d" % (quarter, g))
            nc.sync.dma_start(out=x_piece[quarter, g][:], in_=x_rows(b, g)[:, :, cols])

        def load_m_block(quarter):
            b, cols = pixels_of(quarter)
            m_block[quarter] = keep.tile([P, ROW_TILES, BLOCK], BF16, name="m_%d" % quarter)
            nc.sync.dma_start(out=m_block[quarter][:], in_=m_rows(b)[:, :, cols])

        def load_w_words(half, g):
            nc.sync.dma_start(
                out=w_words[half][:, g, :, :].bitcast(I32),
                in_=Wm_words[g]
                .rearrange("p (a h c) -> p a h c", a=GATES, h=W_HALVES)[:, :, half, :]
                .bitcast(I32),
            )

        for half in range(W_HALVES):
            w_words[half] = keep.tile(
                [P, K_GROUPS, GATES, 2 * C // W_HALVES], U8, align_bytes=64, name="w_words_%d" % half
            )
        for g in range(K_GROUPS):
            load_x_block(0, g)
            if g == 0:
                nc.sync.dma_start(
                    out=bias_rows[0 : 3 * ROW_TILES, :], in_=bm.rearrange("(r c) -> r c", c=P)
                )
                load_w_scales()
            load_w_words(0, g)
        load_m_block(0)
        load_x_block(1, 0)
        for g in range(K_GROUPS):
            load_w_words(1, g)
        for g in range(1, K_GROUPS):
            load_x_block(1, g)
        load_m_block(1)
        for g in range(K_GROUPS):
            x_whole = keep.tile([P, PACK, PIXELS], BF16, name="x_whole_%d" % g)
            nc.sync.dma_start(out=x_whole[:], in_=x_rows(1, g))
            for quarter in range(HALVES, QUARTERS):
                x_piece[quarter, g] = x_whole[:, :, pixels_of(quarter)[1]]
        m_whole = keep.tile([P, ROW_TILES, PIXELS], BF16)
        nc.sync.dma_start(out=m_whole[:], in_=m_rows(1))
        for quarter in range(HALVES, QUARTERS):
            m_block[quarter] = m_whole[:, :, pixels_of(quarter)[1]]

        bias_bank = psum.tile([P, P], BF16, tag="bank")
        nc.tensor.transpose(bias_bank[:], bias_rows[:], identity[:])
        nc.vector.tensor_copy(out=bias[:], in_=bias_bank[:, 0 : 3 * ROW_TILES])

        def regroup_piece(quarter, g):
            grouped = group_pool.tile([P, BLOCK, PACK], BF16, align_bytes=64, name="grouped")
            src = x_piece[quarter, g].rearrange("p t (c i) -> p c t i", i=RUN)
            dst = grouped[:].rearrange("p (c i) t -> p c t i", i=RUN)
            if quarter == 0:
                cut = HEAD_VECTOR_PIXELS // RUN
                nc.vector.tensor_copy(out=dst[:, 0:cut], in_=src[:, 0:cut])
                nc.scalar.copy(out=dst[:, cut:], in_=src[:, cut:])
            else:
                nc.vector.tensor_copy(out=dst, in_=src)
            return grouped, K_GROUPS * quarter + g

        def quantise_piece(grouped, piece):
            nc.vector.quantize_mx(
                out=x_codes[:, piece, :].bitcast(FP8X4),
                scales=x_scales[:, piece, :],
                in_=grouped[:].rearrange("p w t -> p (w t)"),
            )

        def multiply(quarter, j, gate):
            bank = psum.tile([P, BLOCK], F32, tag="bank")
            tile_index = ROW_TILES * gate + j
            for g in range(K_GROUPS):
                piece = K_GROUPS * quarter + g
                nc.tensor.matmul_mx(
                    out=bank[:],
                    lhsT=w_words[j // TILES_PER_HALF][
                        :, g, gate, 2 * P * (j % TILES_PER_HALF) : 2 * P * (j % TILES_PER_HALF + 1)
                    ].bitcast(FP4X4),
                    lhsT_scale=w_scales[:, g, P * tile_index : P * (tile_index + 1)],
                    rhs=x_codes[:, piece, :].bitcast(FP8X4),
                    rhs_scale=x_scales[:, piece, :],
                    start=(g == 0),
                    stop=(g == K_GROUPS - 1),
                )
            return bank

        scalar_chunks = []
        progress = {"chunks": 0}
        copied = []

        def next_scalar_chunk():
            if progress["chunks"] == len(scalar_chunks):
                return
            grouped, quarter, g, c = scalar_chunks[progress["chunks"]]
            progress["chunks"] += 1
            part = slice(c * BLOCK // SCALAR_CHUNKS, (c + 1) * BLOCK // SCALAR_CHUNKS)
            nc.scalar.copy(
                out=grouped[:, part, :].rearrange("p (c i) t -> p c t i", i=RUN),
                in_=x_piece[quarter, g][:, :, part].rearrange("p t (c i) -> p c t i", i=RUN),
            )
            if c == SCALAR_CHUNKS - 1:
                copied.append((grouped, K_GROUPS * quarter + g))

        def activate(bank, j, gate, func, name):
            result = gate_pool.tile([P, BLOCK], F32, name=name)
            column = ROW_TILES * gate + j
            nc.scalar.activation(
                out=result[:], in_=bank[:], func=func, bias=bias[:, column : column + 1], scale=1.0
            )
            next_scalar_chunk()
            return result

        for g in range(K_GROUPS):
            grouped, piece = regroup_piece(0, g)
            quantise_piece(grouped, piece)

        live = {}
        for unit in range(UNITS + 1):
            if unit < UNITS:
                quarter, j = divmod(unit, ROW_TILES)
                b, cols = pixels_of(quarter)
                if unit in SCALAR_FROM_ROUND:
                    grouped = group_pool.tile([P, BLOCK, PACK], BF16, align_bytes=64, name="grouped")
                    for c in range(SCALAR_CHUNKS):
                        scalar_chunks.append((grouped,) + SCALAR_FROM_ROUND[unit] + (c,))
                bank_g = multiply(quarter, j, GATE_G)
                bank_i = multiply(quarter, j, GATE_I)
                bank_o = multiply(quarter, j, GATE_O)
                tanh_g = activate(bank_g, j, GATE_G, ACT.Tanh, "tanh_g")
                sig_i = activate(bank_i, j, GATE_I, ACT.Sigmoid, "sig_i")
                sig_o = activate(bank_o, j, GATE_O, ACT.Sigmoid, "sig_o")
            for grouped, piece in copied:
                quantise_piece(grouped, piece)
            copied.clear()
            if unit < UNITS:
                step = gate_pool.tile([P, BLOCK], F32, name="step")
                nc.vector.tensor_tensor(
                    out=step[:], in0=tanh_g[:], in1=m_block[quarter][:, j, :], op=ALU.subtract
                )
            if unit > 0:
                old = live[unit - 1]
                new_m = gate_pool.tile([P, BLOCK], F32, name="new_m")
                nc.vector.tensor_tensor(out=new_m[:], in0=old["step"][:], in1=old["m"], op=ALU.add)
                nc.sync.dma_start(out=old["out_m"], in_=new_m[:])
            if unit < UNITS:
                if unit in VECTOR_IN_ROUND:
                    copied.append(regroup_piece(VECTOR_IN_ROUND[unit][0], VECTOR_IN_ROUND[unit][1]))
                nc.vector.tensor_tensor(out=step[:], in0=step[:], in1=sig_i[:], op=ALU.mult)
                rows = slice(P * j, P * (j + 1))
                live[unit] = {
                    "step": step,
                    "m": m_block[quarter][:, j, :],
                    "sig_o": sig_o,
                    "out_h": out_0[b, rows].rearrange("p r c -> p (r c)")[:, cols],
                    "out_m": out_1[b, rows].rearrange("p r c -> p (r c)")[:, cols],
                }
            if unit > 0:
                new_h = gate_pool.tile([P, BLOCK], F32, name="new_h")
                parts = LAST_PARTS if unit == UNITS else 1
                for part in range(parts):
                    some = slice(part * BLOCK // parts, (part + 1) * BLOCK // parts)
                    nc.vector.tensor_tensor(
                        out=new_h[:, some], in0=new_m[:, some], in1=old["sig_o"][:, some], op=ALU.mult
                    )
                    nc.sync.dma_start(out=old["out_h"][:, some], in_=new_h[:, some])
